import numpy as np
import ml_dtypes

BF16 = ml_dtypes.bfloat16


def bf(x):
    return np.asarray(x, np.float32).astype(BF16)


def f32(x):
    return np.asarray(x, np.float32)


def f64(x):
    return np.asarray(x).astype(np.float64)


def striped(idx):
    return np.tile(idx.reshape(-1, 16).T, (8, 1))


C, S, N, H = 256, 1024, 512, 128
BASE = 10000.0
EMB_SCALE = 0.5


def rotary_tables():
    inv = np.float32(1.0) / np.power(np.float32(BASE), np.arange(H, dtype=np.float32) / np.float32(H))
    ang = inv[:, None] * np.arange(N, dtype=np.float32)[None, :]
    co, si = np.cos(f64(ang)), np.sin(f64(ang))
    return f32(np.concatenate([co, co], axis=0)), f32(np.concatenate([-si, si], axis=0))


def setup_inputs():
    cos_pos, sin_pos = rotary_tables()
    return {"emb": f32(EMB_SCALE * np.random.standard_normal((C, S))), "cos_pos": cos_pos, "sin_pos": sin_pos, "offs": striped(np.random.permutation(np.tile(np.arange(S), 2))[:N])}


def reference(emb, cos_pos, sin_pos, offs):
    idx = offs[:16].T.reshape(-1)
    t = f64(emb)[:, idx]
    return t * f64(cos_pos) + np.roll(t, H, axis=0) * f64(sin_pos)

@@ -1,0 +1,42 @@
+import concourse.mybir as mybir
+
+F32 = mybir.dt.float32
+U16 = mybir.dt.uint16
+MULT = mybir.AluOpType.mult
+ADD = mybir.AluOpType.add
+
+P = 128
+BLOCKS = 2
+
+
+def tile_progen_kernel(tc, emb, cos_pos, sin_pos, offs, out):
+    nc = tc.nc
+    words = emb.shape[1]
+    tokens = out.shape[1]
+
+    with tc.tile_pool(name="held", bufs=1) as held:
+        offsets = held.tile([P, tokens // 16], U16, name="offsets")
+        nc.sync.dma_start(offsets[:], offs)
+
+        table, cosines, sines = {}, {}, {}
+        for t in range(BLOCKS):
+            rows_t = slice(t * P, (t + 1) * P)
+            rows_other = slice((1 - t) * P, (2 - t) * P)
+            table[t] = held.tile([P, words], F32, name=f"table{t}")
+            cosines[t] = held.tile([P, tokens], F32, name=f"cosines{t}")
+            sines[1 - t] = held.tile([P, tokens], F32, name=f"sines{1 - t}")
+            nc.sync.dma_start(table[t][:], emb[rows_t, :])
+            nc.sync.dma_start(cosines[t][:], cos_pos[rows_t, :])
+            nc.sync.dma_start(sines[1 - t][:], sin_pos[rows_other, :])
+
+        straight, rotated = {}, {}
+        for t in range(BLOCKS):
+            looked_up = table[t][:].indirect(offsets[:])
+            straight[t] = held.tile([P, tokens], F32, name=f"straight{t}")
+            rotated[1 - t] = held.tile([P, tokens], F32, name=f"rotated{1 - t}")
+            nc.vector.tensor_tensor(straight[t][:], looked_up, cosines[t][:], MULT)
+            nc.vector.tensor_tensor(rotated[1 - t][:], looked_up, sines[1 - t][:], MULT)
+
+        for b in range(BLOCKS):
+            nc.vector.tensor_tensor(straight[b][:], straight[b][:], rotated[b][:], ADD)
+            nc.sync.dma_start(out[b * P : (b + 1) * P, :], straight[b][:])

@@ -7,36 +7,43 @@ ADD = mybir.AluOpType.add
 
 P = 128
 BLOCKS = 2
+HALVES = 2
 
 
 def tile_progen_kernel(tc, emb, cos_pos, sin_pos, offs, out):
     nc = tc.nc
     words = emb.shape[1]
     tokens = out.shape[1]
+    half = tokens // HALVES
 
     with tc.tile_pool(name="held", bufs=1) as held:
         offsets = held.tile([P, tokens // 16], U16, name="offsets")
         nc.sync.dma_start(offsets[:], offs)
 
-        table, cosines, sines = {}, {}, {}
+        table, factor, product = {}, {}, {}
         for t in range(BLOCKS):
-            rows_t = slice(t * P, (t + 1) * P)
-            rows_other = slice((1 - t) * P, (2 - t) * P)
             table[t] = held.tile([P, words], F32, name=f"table{t}")
-            cosines[t] = held.tile([P, tokens], F32, name=f"cosines{t}")
-            sines[1 - t] = held.tile([P, tokens], F32, name=f"sines{1 - t}")
-            nc.sync.dma_start(table[t][:], emb[rows_t, :])
-            nc.sync.dma_start(cosines[t][:], cos_pos[rows_t, :])
-            nc.sync.dma_start(sines[1 - t][:], sin_pos[rows_other, :])
+            nc.sync.dma_start(table[t][:], emb[t * P : (t + 1) * P, :])
+            for b in range(BLOCKS):
+                source = cos_pos if b == t else sin_pos
+                factor[t, b] = held.tile([P, tokens], F32, name=f"factor{t}{b}")
+                product[t, b] = held.tile([P, tokens], F32, name=f"product{t}{b}")
+                if (t, b) == (0, 0):
+                    for h in range(HALVES):
+                        cols = slice(h * half, (h + 1) * half)
+                        nc.sync.dma_start(factor[t, b][:, cols], source[b * P : (b + 1) * P, cols])
+                else:
+                    nc.sync.dma_start(factor[t, b][:], source[b * P : (b + 1) * P, :])
 
-        straight, rotated = {}, {}
-        for t in range(BLOCKS):
-            looked_up = table[t][:].indirect(offsets[:])
-            straight[t] = held.tile([P, tokens], F32, name=f"straight{t}")
-            rotated[1 - t] = held.tile([P, tokens], F32, name=f"rotated{1 - t}")
-            nc.vector.tensor_tensor(straight[t][:], looked_up, cosines[t][:], MULT)
-            nc.vector.tensor_tensor(rotated[1 - t][:], looked_up, sines[1 - t][:], MULT)
+        for h in range(HALVES):
+            cols = slice(h * half, (h + 1) * half)
+            looked_up = table[0][:].indirect(offsets[:, h * half // 16 : (h + 1) * half // 16])
+            nc.vector.tensor_tensor(product[0, 0][:, cols], looked_up, factor[0, 0][:, cols], MULT)
+        for t, b in ((0, 1), (1, 0), (1, 1)):
+            nc.vector.tensor_tensor(product[t, b][:], table[t][:].indirect(offsets[:]), factor[t, b][:], MULT)
 
         for b in range(BLOCKS):
-            nc.vector.tensor_tensor(straight[b][:], straight[b][:], rotated[b][:], ADD)
-            nc.sync.dma_start(out[b * P : (b + 1) * P, :], straight[b][:])
+            for h in range(HALVES):
+                cols = slice(h * half, (h + 1) * half)
+                nc.vector.tensor_tensor(product[0, b][:, cols], product[0, b][:, cols], product[1, b][:, cols], ADD)
+                nc.sync.dma_start(out[b * P : (b + 1) * P, cols], product[0, b][:, cols])

@@ -35,15 +35,22 @@ def tile_progen_kernel(tc, emb, cos_pos, sin_pos, offs, out):
                 else:
                     nc.sync.dma_start(factor[t, b][:], source[b * P : (b + 1) * P, :])
 
-        for h in range(HALVES):
-            cols = slice(h * half, (h + 1) * half)
-            looked_up = table[0][:].indirect(offsets[:, h * half // 16 : (h + 1) * half // 16])
-            nc.vector.tensor_tensor(product[0, 0][:, cols], looked_up, factor[0, 0][:, cols], MULT)
-        for t, b in ((0, 1), (1, 0), (1, 1)):
+        def multiply_whole(t, b):
             nc.vector.tensor_tensor(product[t, b][:], table[t][:].indirect(offsets[:]), factor[t, b][:], MULT)
 
-        for b in range(BLOCKS):
+        def multiply_halves(t, b):
             for h in range(HALVES):
                 cols = slice(h * half, (h + 1) * half)
-                nc.vector.tensor_tensor(product[0, b][:, cols], product[0, b][:, cols], product[1, b][:, cols], ADD)
-                nc.sync.dma_start(out[b * P : (b + 1) * P, cols], product[0, b][:, cols])
+                looked_up = table[t][:].indirect(offsets[:, h * half // 16 : (h + 1) * half // 16])
+                nc.vector.tensor_tensor(product[t, b][:, cols], looked_up, factor[t, b][:, cols], MULT)
+
+        multiply_halves(0, 0)
+        multiply_whole(0, 1)
+        multiply_whole(1, 0)
+        nc.gpsimd.tensor_tensor(product[0, 0][:], product[0, 0][:], product[1, 0][:], ADD)
+        nc.sync.dma_start(out[0:P, :], product[0, 0][:])
+        multiply_halves(1, 1)
+        for h in range(HALVES):
+            cols = slice(h * half, (h + 1) * half)
+            nc.vector.tensor_tensor(product[0, 1][:, cols], product[0, 1][:, cols], product[1, 1][:, cols], ADD)
+            nc.sync.dma_start(out[P : 2 * P, cols], product[0, 1][:, cols])

@@ -23,7 +23,7 @@ def tile_progen_kernel(tc, emb, cos_pos, sin_pos, offs, out):
         table, factor, product = {}, {}, {}
         for t in range(BLOCKS):
             table[t] = held.tile([P, words], F32, name=f"table{t}")
-            nc.sync.dma_start(table[t][:], emb[t * P : (t + 1) * P, :])
+            nc.scalar.dma_start(table[t][:], emb[t * P : (t + 1) * P, :])
             for b in range(BLOCKS):
                 source = cos_pos if b == t else sin_pos
                 factor[t, b] = held.tile([P, tokens], F32, name=f"factor{t}{b}")
@@ -31,26 +31,19 @@ def tile_progen_kernel(tc, emb, cos_pos, sin_pos, offs, out):
                 if (t, b) == (0, 0):
                     for h in range(HALVES):
                         cols = slice(h * half, (h + 1) * half)
-                        nc.sync.dma_start(factor[t, b][:, cols], source[b * P : (b + 1) * P, cols])
+                        nc.scalar.dma_start(factor[t, b][:, cols], source[b * P : (b + 1) * P, cols])
                 else:
-                    nc.sync.dma_start(factor[t, b][:], source[b * P : (b + 1) * P, :])
+                    nc.scalar.dma_start(factor[t, b][:], source[b * P : (b + 1) * P, :])
 
-        def multiply_whole(t, b):
-            nc.vector.tensor_tensor(product[t, b][:], table[t][:].indirect(offsets[:]), factor[t, b][:], MULT)
-
-        def multiply_halves(t, b):
-            for h in range(HALVES):
-                cols = slice(h * half, (h + 1) * half)
-                looked_up = table[t][:].indirect(offsets[:, h * half // 16 : (h + 1) * half // 16])
-                nc.vector.tensor_tensor(product[t, b][:, cols], looked_up, factor[t, b][:, cols], MULT)
-
-        multiply_halves(0, 0)
-        multiply_whole(0, 1)
-        multiply_whole(1, 0)
-        nc.gpsimd.tensor_tensor(product[0, 0][:], product[0, 0][:], product[1, 0][:], ADD)
-        nc.sync.dma_start(out[0:P, :], product[0, 0][:])
-        multiply_halves(1, 1)
         for h in range(HALVES):
             cols = slice(h * half, (h + 1) * half)
-            nc.vector.tensor_tensor(product[0, 1][:, cols], product[0, 1][:, cols], product[1, 1][:, cols], ADD)
-            nc.sync.dma_start(out[P : 2 * P, cols], product[0, 1][:, cols])
+            looked_up = table[0][:].indirect(offsets[:, h * half // 16 : (h + 1) * half // 16])
+            nc.vector.tensor_tensor(product[0, 0][:, cols], looked_up, factor[0, 0][:, cols], MULT)
+        for t, b in ((0, 1), (1, 0), (1, 1)):
+            nc.vector.tensor_tensor(product[t, b][:], table[t][:].indirect(offsets[:]), factor[t, b][:], MULT)
+
+        for b in range(BLOCKS):
+            for h in range(HALVES):
+                cols = slice(h * half, (h + 1) * half)
+                nc.vector.tensor_tensor(product[0, b][:, cols], product[0, b][:, cols], product[1, b][:, cols], ADD)
+                nc.sync.dma_start(out[b * P : (b + 1) * P, cols], product[0, b][:, cols])

@@ -7,6 +7,7 @@ ADD = mybir.AluOpType.add
 
 P = 128
 BLOCKS = 2
+OFFSETS_PER_COLUMN = 16
 HALVES = 2
 
 
@@ -14,36 +15,50 @@ def tile_progen_kernel(tc, emb, cos_pos, sin_pos, offs, out):
     nc = tc.nc
     words = emb.shape[1]
     tokens = out.shape[1]
-    half = tokens // HALVES
+
+    def rows(block):
+        return slice(block * P, (block + 1) * P)
+
+    def token_cols(k, pieces):
+        width = tokens // pieces
+        return slice(k * width, (k + 1) * width)
+
+    def offset_cols(k, pieces):
+        width = tokens // pieces // OFFSETS_PER_COLUMN
+        return slice(k * width, (k + 1) * width)
+
+    def pieces_of_product(t, b):
+        return HALVES if (t, b) == (0, 0) else 1
 
     with tc.tile_pool(name="held", bufs=1) as held:
-        offsets = held.tile([P, tokens // 16], U16, name="offsets")
+        offsets = held.tile([P, tokens // OFFSETS_PER_COLUMN], U16, name="offsets")
         nc.sync.dma_start(offsets[:], offs)
 
-        table, factor, product = {}, {}, {}
+        table, factor = {}, {}
         for t in range(BLOCKS):
             table[t] = held.tile([P, words], F32, name=f"table{t}")
-            nc.scalar.dma_start(table[t][:], emb[t * P : (t + 1) * P, :])
+            nc.sync.dma_start(table[t][:], emb[rows(t), :])
             for b in range(BLOCKS):
-                source = cos_pos if b == t else sin_pos
+                angles = cos_pos if b == t else sin_pos
                 factor[t, b] = held.tile([P, tokens], F32, name=f"factor{t}{b}")
-                product[t, b] = held.tile([P, tokens], F32, name=f"product{t}{b}")
-                if (t, b) == (0, 0):
-                    for h in range(HALVES):
-                        cols = slice(h * half, (h + 1) * half)
-                        nc.scalar.dma_start(factor[t, b][:, cols], source[b * P : (b + 1) * P, cols])
-                else:
-                    nc.scalar.dma_start(factor[t, b][:], source[b * P : (b + 1) * P, :])
+                pieces = pieces_of_product(t, b)
+                for k in range(pieces):
+                    cols = token_cols(k, pieces)
+                    nc.sync.dma_start(factor[t, b][:, cols], angles[rows(b), cols])
 
-        for h in range(HALVES):
-            cols = slice(h * half, (h + 1) * half)
-            looked_up = table[0][:].indirect(offsets[:, h * half // 16 : (h + 1) * half // 16])
-            nc.vector.tensor_tensor(product[0, 0][:, cols], looked_up, factor[0, 0][:, cols], MULT)
-        for t, b in ((0, 1), (1, 0), (1, 1)):
-            nc.vector.tensor_tensor(product[t, b][:], table[t][:].indirect(offsets[:]), factor[t, b][:], MULT)
+        product = {}
+        for t in range(BLOCKS):
+            for b in range(BLOCKS):
+                product[t, b] = held.tile([P, tokens], F32, name=f"product{t}{b}")
+                pieces = pieces_of_product(t, b)
+                for k in range(pieces):
+                    cols = token_cols(k, pieces)
+                    looked_up = table[t][:].indirect(offsets[:, offset_cols(k, pieces)])
+                    nc.vector.tensor_tensor(product[t, b][:, cols], looked_up, factor[t, b][:, cols], MULT)
 
         for b in range(BLOCKS):
-            for h in range(HALVES):
-                cols = slice(h * half, (h + 1) * half)
-                nc.vector.tensor_tensor(product[0, b][:, cols], product[0, b][:, cols], product[1, b][:, cols], ADD)
-                nc.sync.dma_start(out[b * P : (b + 1) * P, cols], product[0, b][:, cols])
+            turned = held.tile([P, tokens], F32, name=f"turned{b}")
+            for k in range(HALVES):
+                cols = token_cols(k, HALVES)
+                nc.vector.tensor_tensor(turned[:, cols], product[0, b][:, cols], product[1, b][:, cols], ADD)
+                nc.sync.dma_start(out[rows(b), cols], turned[:, cols])

@@ -28,7 +28,7 @@ def tile_progen_kernel(tc, emb, cos_pos, sin_pos, offs, out):
         return slice(k * width, (k + 1) * width)
 
     def pieces_of_product(t, b):
-        return HALVES if (t, b) == (0, 0) else 1
+        return HALVES if b == 0 else 1
 
     with tc.tile_pool(name="held", bufs=1) as held:
         offsets = held.tile([P, tokens // OFFSETS_PER_COLUMN], U16, name="offsets")

@@ -15,20 +15,10 @@ def tile_progen_kernel(tc, emb, cos_pos, sin_pos, offs, out):
     nc = tc.nc
     words = emb.shape[1]
     tokens = out.shape[1]
+    half = tokens // HALVES
 
     def rows(block):
         return slice(block * P, (block + 1) * P)
-
-    def token_cols(k, pieces):
-        width = tokens // pieces
-        return slice(k * width, (k + 1) * width)
-
-    def offset_cols(k, pieces):
-        width = tokens // pieces // OFFSETS_PER_COLUMN
-        return slice(k * width, (k + 1) * width)
-
-    def pieces_of_product(t, b):
-        return HALVES if b == 0 else 1
 
     with tc.tile_pool(name="held", bufs=1) as held:
         offsets = held.tile([P, tokens // OFFSETS_PER_COLUMN], U16, name="offsets")
@@ -41,24 +31,18 @@ def tile_progen_kernel(tc, emb, cos_pos, sin_pos, offs, out):
             for b in range(BLOCKS):
                 angles = cos_pos if b == t else sin_pos
                 factor[t, b] = held.tile([P, tokens], F32, name=f"factor{t}{b}")
-                pieces = pieces_of_product(t, b)
-                for k in range(pieces):
-                    cols = token_cols(k, pieces)
-                    nc.sync.dma_start(factor[t, b][:, cols], angles[rows(b), cols])
+                nc.sync.dma_start(factor[t, b][:], angles[rows(b), :])
 
         product = {}
         for t in range(BLOCKS):
             for b in range(BLOCKS):
                 product[t, b] = held.tile([P, tokens], F32, name=f"product{t}{b}")
-                pieces = pieces_of_product(t, b)
-                for k in range(pieces):
-                    cols = token_cols(k, pieces)
-                    looked_up = table[t][:].indirect(offsets[:, offset_cols(k, pieces)])
-                    nc.vector.tensor_tensor(product[t, b][:, cols], looked_up, factor[t, b][:, cols], MULT)
+                looked_up = table[t][:].indirect(offsets[:])
+                nc.vector.tensor_tensor(product[t, b][:], looked_up, factor[t, b][:], MULT)
 
         for b in range(BLOCKS):
             turned = held.tile([P, tokens], F32, name=f"turned{b}")
-            for k in range(HALVES):
-                cols = token_cols(k, HALVES)
+            for h in range(HALVES):
+                cols = slice(h * half, (h + 1) * half)
                 nc.vector.tensor_tensor(turned[:, cols], product[0, b][:, cols], product[1, b][:, cols], ADD)
                 nc.sync.dma_start(out[rows(b), cols], turned[:, cols])

@@ -22,12 +22,13 @@ def tile_progen_kernel(tc, emb, cos_pos, sin_pos, offs, out):
 
     with tc.tile_pool(name="held", bufs=1) as held:
         offsets = held.tile([P, tokens // OFFSETS_PER_COLUMN], U16, name="offsets")
-        nc.sync.dma_start(offsets[:], offs)
 
         table, factor = {}, {}
         for t in range(BLOCKS):
             table[t] = held.tile([P, words], F32, name=f"table{t}")
             nc.sync.dma_start(table[t][:], emb[rows(t), :])
+            if t == 0:
+                nc.sync.dma_start(offsets[:], offs)
             for b in range(BLOCKS):
                 angles = cos_pos if b == t else sin_pos
                 factor[t, b] = held.tile([P, tokens], F32, name=f"factor{t}{b}")

@@ -9,6 +9,7 @@ P = 128
 BLOCKS = 2
 OFFSETS_PER_COLUMN = 16
 HALVES = 2
+HEAD = 128
 
 
 def tile_progen_kernel(tc, emb, cos_pos, sin_pos, offs, out):
@@ -16,6 +17,7 @@ def tile_progen_kernel(tc, emb, cos_pos, sin_pos, offs, out):
     words = emb.shape[1]
     tokens = out.shape[1]
     half = tokens // HALVES
+    head, rest, whole = slice(0, HEAD), slice(HEAD, tokens), slice(0, tokens)
 
     def rows(block):
         return slice(block * P, (block + 1) * P)
@@ -23,23 +25,27 @@ def tile_progen_kernel(tc, emb, cos_pos, sin_pos, offs, out):
     with tc.tile_pool(name="held", bufs=1) as held:
         offsets = held.tile([P, tokens // OFFSETS_PER_COLUMN], U16, name="offsets")
 
-        table, factor = {}, {}
+        table = [held.tile([P, words], F32, name=f"table{t}") for t in range(BLOCKS)]
+        factor = {(t, b): held.tile([P, tokens], F32, name=f"factor{t}{b}") for t in range(BLOCKS) for b in range(BLOCKS)}
+
+        def load_factor(t, b, cols):
+            angles = cos_pos if b == t else sin_pos
+            nc.sync.dma_start(factor[t, b][:, cols], angles[rows(b), cols])
+
         for t in range(BLOCKS):
-            table[t] = held.tile([P, words], F32, name=f"table{t}")
+            load_factor(t, 0, head)
             nc.sync.dma_start(table[t][:], emb[rows(t), :])
             if t == 0:
                 nc.sync.dma_start(offsets[:], offs)
-            for b in range(BLOCKS):
-                angles = cos_pos if b == t else sin_pos
-                factor[t, b] = held.tile([P, tokens], F32, name=f"factor{t}{b}")
-                nc.sync.dma_start(factor[t, b][:], angles[rows(b), :])
+            load_factor(t, 0, rest)
+            load_factor(t, 1, whole)
 
-        product = {}
+        product = {(t, b): held.tile([P, tokens], F32, name=f"product{t}{b}") for t in range(BLOCKS) for b in range(BLOCKS)}
         for t in range(BLOCKS):
-            for b in range(BLOCKS):
-                product[t, b] = held.tile([P, tokens], F32, name=f"product{t}{b}")
-                looked_up = table[t][:].indirect(offsets[:])
-                nc.vector.tensor_tensor(product[t, b][:], looked_up, factor[t, b][:], MULT)
+            for b, cols in ((0, head), (0, rest), (1, whole)):
+                listed = offsets[:, cols.start // OFFSETS_PER_COLUMN : cols.stop // OFFSETS_PER_COLUMN]
+                looked_up = table[t][:].indirect(listed)
+                nc.vector.tensor_tensor(product[t, b][:, cols], looked_up, factor[t, b][:, cols], MULT)
 
         for b in range(BLOCKS):
             turned = held.tile([P, tokens], F32, name=f"turned{b}")

@@ -1,4 +1,5 @@
 import concourse.mybir as mybir
+from concourse.masks import make_identity
 
 F32 = mybir.dt.float32
 U16 = mybir.dt.uint16
@@ -10,6 +11,7 @@ BLOCKS = 2
 OFFSETS_PER_COLUMN = 16
 HALVES = 2
 HEAD = 128
+FLOPS = 3 * 256 * 512
 
 
 def tile_progen_kernel(tc, emb, cos_pos, sin_pos, offs, out):
@@ -17,12 +19,18 @@ def tile_progen_kernel(tc, emb, cos_pos, sin_pos, offs, out):
     words = emb.shape[1]
     tokens = out.shape[1]
     half = tokens // HALVES
-    head, rest, whole = slice(0, HEAD), slice(HEAD, tokens), slice(0, tokens)
+    halves = [slice(h * half, (h + 1) * half) for h in range(HALVES)]
+    whole = slice(0, tokens)
+
+    pieces = [
+        [(0, slice(0, HEAD)), (0, slice(HEAD, tokens)), (1, whole)],
+        [(0, halves[0]), (0, halves[1]), (1, halves[0]), (1, halves[1])],
+    ]
 
     def rows(block):
         return slice(block * P, (block + 1) * P)
 
-    with tc.tile_pool(name="held", bufs=1) as held:
+    with tc.tile_pool(name="held", bufs=1) as held, tc.psum_pool(name="banks", bufs=1) as banks:
         offsets = held.tile([P, tokens // OFFSETS_PER_COLUMN], U16, name="offsets")
 
         table = [held.tile([P, words], F32, name=f"table{t}") for t in range(BLOCKS)]
@@ -33,23 +41,45 @@ def tile_progen_kernel(tc, emb, cos_pos, sin_pos, offs, out):
             nc.sync.dma_start(factor[t, b][:, cols], angles[rows(b), cols])
 
         for t in range(BLOCKS):
-            load_factor(t, 0, head)
+            load_factor(t, *pieces[t][0])
             nc.sync.dma_start(table[t][:], emb[rows(t), :])
             if t == 0:
                 nc.sync.dma_start(offsets[:], offs)
-            load_factor(t, 0, rest)
-            load_factor(t, 1, whole)
+            for b, cols in pieces[t][1:]:
+                load_factor(t, b, cols)
 
+        identity = held.tile([P, P], F32, name="identity")
+        make_identity(nc, identity[:])
+
+        bank = banks.tile([P, half], F32, name="bank")
         product = {(t, b): held.tile([P, tokens], F32, name=f"product{t}{b}") for t in range(BLOCKS) for b in range(BLOCKS)}
-        for t in range(BLOCKS):
-            for b, cols in ((0, head), (0, rest), (1, whole)):
-                listed = offsets[:, cols.start // OFFSETS_PER_COLUMN : cols.stop // OFFSETS_PER_COLUMN]
-                looked_up = table[t][:].indirect(listed)
-                nc.vector.tensor_tensor(product[t, b][:, cols], looked_up, factor[t, b][:, cols], MULT)
+        turned = [held.tile([P, tokens], F32, name=f"turned{b}") for b in range(BLOCKS)]
 
-        for b in range(BLOCKS):
-            turned = held.tile([P, tokens], F32, name=f"turned{b}")
-            for h in range(HALVES):
-                cols = slice(h * half, (h + 1) * half)
-                nc.vector.tensor_tensor(turned[:, cols], product[0, b][:, cols], product[1, b][:, cols], ADD)
-                nc.sync.dma_start(out[rows(b), cols], turned[:, cols])
+        def multiply(t, b, cols):
+            listed = offsets[:, cols.start // OFFSETS_PER_COLUMN : cols.stop // OFFSETS_PER_COLUMN]
+            looked_up = table[t][:].indirect(listed)
+            nc.vector.tensor_tensor(product[t, b][:, cols], looked_up, factor[t, b][:, cols], MULT)
+
+        def add_on_tensor(t):
+            nc.tensor.matmul(
+                bank[:], identity[:], product[t, 0][:, halves[0]], start=(t == 0), stop=(t == BLOCKS - 1)
+            )
+
+        def add_on_vector(b, cols):
+            nc.vector.tensor_tensor(turned[b][:, cols], product[0, b][:, cols], product[1, b][:, cols], ADD)
+            nc.sync.dma_start(out[rows(b), cols], turned[b][:, cols])
+
+        for b, cols in pieces[0]:
+            multiply(0, b, cols)
+        add_on_tensor(0)
+
+        multiply(1, 0, halves[0])
+        add_on_tensor(1)
+        nc.scalar.copy(turned[0][:, halves[0]], bank[:])
+        nc.scalar.dma_start(out[rows(0), halves[0]], turned[0][:, halves[0]])
+        multiply(1, 0, halves[1])
+        multiply(1, 1, halves[0])
+        multiply(1, 1, halves[1])
+        add_on_vector(0, halves[1])
+        add_on_vector(1, halves[0])
+        add_on_vector(1, halves[1])

@@ -9,7 +9,6 @@ ADD = mybir.AluOpType.add
 P = 128
 BLOCKS = 2
 OFFSETS_PER_COLUMN = 16
-HALVES = 2
 HEAD = 128
 FLOPS = 3 * 256 * 512
 
@@ -18,13 +17,13 @@ def tile_progen_kernel(tc, emb, cos_pos, sin_pos, offs, out):
     nc = tc.nc
     words = emb.shape[1]
     tokens = out.shape[1]
-    half = tokens // HALVES
-    halves = [slice(h * half, (h + 1) * half) for h in range(HALVES)]
-    whole = slice(0, tokens)
+    half = tokens // 2
+    head, rest, whole = slice(0, HEAD), slice(HEAD, tokens), slice(0, tokens)
+    first_half, second_half = slice(0, half), slice(half, tokens)
 
     pieces = [
-        [(0, slice(0, HEAD)), (0, slice(HEAD, tokens)), (1, whole)],
-        [(0, halves[0]), (0, halves[1]), (1, halves[0]), (1, halves[1])],
+        [(0, head), (0, rest), (1, whole)],
+        [(0, head), (0, rest), (1, first_half), (1, second_half)],
     ]
 
     def rows(block):
@@ -51,35 +50,18 @@ def tile_progen_kernel(tc, emb, cos_pos, sin_pos, offs, out):
         identity = held.tile([P, P], F32, name="identity")
         make_identity(nc, identity[:])
 
-        bank = banks.tile([P, half], F32, name="bank")
+        bank = banks.tile([P, HEAD], F32, name="bank")
         product = {(t, b): held.tile([P, tokens], F32, name=f"product{t}{b}") for t in range(BLOCKS) for b in range(BLOCKS)}
+        for t in range(BLOCKS):
+            for b, cols in pieces[t]:
+                listed = offsets[:, cols.start // OFFSETS_PER_COLUMN : cols.stop // OFFSETS_PER_COLUMN]
+                looked_up = table[t][:].indirect(listed)
+                nc.vector.tensor_tensor(product[t, b][:, cols], looked_up, factor[t, b][:, cols], MULT)
+            nc.tensor.matmul(bank[:], identity[:], product[t, 0][:, head], start=(t == 0), stop=(t == BLOCKS - 1))
+
         turned = [held.tile([P, tokens], F32, name=f"turned{b}") for b in range(BLOCKS)]
-
-        def multiply(t, b, cols):
-            listed = offsets[:, cols.start // OFFSETS_PER_COLUMN : cols.stop // OFFSETS_PER_COLUMN]
-            looked_up = table[t][:].indirect(listed)
-            nc.vector.tensor_tensor(product[t, b][:, cols], looked_up, factor[t, b][:, cols], MULT)
-
-        def add_on_tensor(t):
-            nc.tensor.matmul(
-                bank[:], identity[:], product[t, 0][:, halves[0]], start=(t == 0), stop=(t == BLOCKS - 1)
-            )
-
-        def add_on_vector(b, cols):
+        nc.scalar.copy(turned[0][:, head], bank[:])
+        nc.scalar.dma_start(out[rows(0), head], turned[0][:, head])
+        for b, cols in ((0, rest), (1, first_half), (1, second_half)):
             nc.vector.tensor_tensor(turned[b][:, cols], product[0, b][:, cols], product[1, b][:, cols], ADD)
             nc.sync.dma_start(out[rows(b), cols], turned[b][:, cols])
-
-        for b, cols in pieces[0]:
-            multiply(0, b, cols)
-        add_on_tensor(0)
-
-        multiply(1, 0, halves[0])
-        add_on_tensor(1)
-        nc.scalar.copy(turned[0][:, halves[0]], bank[:])
-        nc.scalar.dma_start(out[rows(0), halves[0]], turned[0][:, halves[0]])
-        multiply(1, 0, halves[1])
-        multiply(1, 1, halves[0])
-        multiply(1, 1, halves[1])
-        add_on_vector(0, halves[1])
-        add_on_vector(1, halves[0])
-        add_on_vector(1, halves[1])

@@ -10,6 +10,7 @@ P = 128
 BLOCKS = 2
 OFFSETS_PER_COLUMN = 16
 HEAD = 128
+SHARES = 2
 FLOPS = 3 * 256 * 512
 
 
@@ -20,10 +21,12 @@ def tile_progen_kernel(tc, emb, cos_pos, sin_pos, offs, out):
     half = tokens // 2
     head, rest, whole = slice(0, HEAD), slice(HEAD, tokens), slice(0, tokens)
     first_half, second_half = slice(0, half), slice(half, tokens)
+    shares = [slice(k * HEAD, (k + 1) * HEAD) for k in range(SHARES)]
+    left = slice(SHARES * HEAD, tokens)
 
     pieces = [
         [(0, head), (0, rest), (1, whole)],
-        [(0, head), (0, rest), (1, first_half), (1, second_half)],
+        [(0, cols) for cols in shares] + [(1, whole), (0, left)],
     ]
 
     def rows(block):
@@ -50,18 +53,22 @@ def tile_progen_kernel(tc, emb, cos_pos, sin_pos, offs, out):
         identity = held.tile([P, P], F32, name="identity")
         make_identity(nc, identity[:])
 
-        bank = banks.tile([P, HEAD], F32, name="bank")
+        bank = [banks.tile([P, HEAD], F32, name=f"bank{k}") for k in range(SHARES)]
         product = {(t, b): held.tile([P, tokens], F32, name=f"product{t}{b}") for t in range(BLOCKS) for b in range(BLOCKS)}
         for t in range(BLOCKS):
             for b, cols in pieces[t]:
                 listed = offsets[:, cols.start // OFFSETS_PER_COLUMN : cols.stop // OFFSETS_PER_COLUMN]
                 looked_up = table[t][:].indirect(listed)
                 nc.vector.tensor_tensor(product[t, b][:, cols], looked_up, factor[t, b][:, cols], MULT)
-            nc.tensor.matmul(bank[:], identity[:], product[t, 0][:, head], start=(t == 0), stop=(t == BLOCKS - 1))
+            for k in range(SHARES):
+                nc.tensor.matmul(
+                    bank[k][:], identity[:], product[t, 0][:, shares[k]], start=(t == 0), stop=(t == BLOCKS - 1)
+                )
 
         turned = [held.tile([P, tokens], F32, name=f"turned{b}") for b in range(BLOCKS)]
-        nc.scalar.copy(turned[0][:, head], bank[:])
-        nc.scalar.dma_start(out[rows(0), head], turned[0][:, head])
-        for b, cols in ((0, rest), (1, first_half), (1, second_half)):
+        for k in range(SHARES):
+            nc.scalar.copy(turned[0][:, shares[k]], bank[k][:])
+            nc.scalar.dma_start(out[rows(0), shares[k]], turned[0][:, shares[k]])
+        for b, cols in ((1, first_half), (1, second_half), (0, left)):
             nc.vector.tensor_tensor(turned[b][:, cols], product[0, b][:, cols], product[1, b][:, cols], ADD)
             nc.sync.dma_start(out[rows(b), cols], turned[b][:, cols])

@@ -68,7 +68,7 @@ def tile_progen_kernel(tc, emb, cos_pos, sin_pos, offs, out):
         turned = [held.tile([P, tokens], F32, name=f"turned{b}") for b in range(BLOCKS)]
         for k in range(SHARES):
             nc.scalar.copy(turned[0][:, shares[k]], bank[k][:])
-            nc.scalar.dma_start(out[rows(0), shares[k]], turned[0][:, shares[k]])
+            nc.sync.dma_start(out[rows(0), shares[k]], turned[0][:, shares[k]])
         for b, cols in ((1, first_half), (1, second_half), (0, left)):
             nc.vector.tensor_tensor(turned[b][:, cols], product[0, b][:, cols], product[1, b][:, cols], ADD)
-            nc.sync.dma_start(out[rows(b), cols], turned[b][:, cols])
+            nc.scalar.dma_start(out[rows(b), cols], turned[b][:, cols])

import concourse.mybir as mybir
from concourse.masks import make_identity

F32 = mybir.dt.float32
U16 = mybir.dt.uint16
MULT = mybir.AluOpType.mult
ADD = mybir.AluOpType.add

P = 128
BLOCKS = 2
OFFSETS_PER_COLUMN = 16
HEAD = 128
SHARES = 2
FLOPS = 3 * 256 * 512


def tile_progen_kernel(tc, emb, cos_pos, sin_pos, offs, out):
    nc = tc.nc
    words = emb.shape[1]
    tokens = out.shape[1]
    half = tokens // 2
    head, rest, whole = slice(0, HEAD), slice(HEAD, tokens), slice(0, tokens)
    first_half, second_half = slice(0, half), slice(half, tokens)
    shares = [slice(k * HEAD, (k + 1) * HEAD) for k in range(SHARES)]
    left = slice(SHARES * HEAD, tokens)

    pieces = [
        [(0, head), (0, rest), (1, whole)],
        [(0, cols) for cols in shares] + [(1, whole), (0, left)],
    ]

    def rows(block):
        return slice(block * P, (block + 1) * P)

    with tc.tile_pool(name="held", bufs=1) as held, tc.psum_pool(name="banks", bufs=1) as banks:
        offsets = held.tile([P, tokens // OFFSETS_PER_COLUMN], U16, name="offsets")

        table = [held.tile([P, words], F32, name=f"table{t}") for t in range(BLOCKS)]
        factor = {(t, b): held.tile([P, tokens], F32, name=f"factor{t}{b}") for t in range(BLOCKS) for b in range(BLOCKS)}

        def load_factor(t, b, cols):
            angles = cos_pos if b == t else sin_pos
            nc.sync.dma_start(factor[t, b][:, cols], angles[rows(b), cols])

        for t in range(BLOCKS):
            load_factor(t, *pieces[t][0])
            nc.sync.dma_start(table[t][:], emb[rows(t), :])
            if t == 0:
                nc.sync.dma_start(offsets[:], offs)
            for b, cols in pieces[t][1:]:
                load_factor(t, b, cols)

        identity = held.tile([P, P], F32, name="identity")
        make_identity(nc, identity[:])

        bank = [banks.tile([P, HEAD], F32, name=f"bank{k}") for k in range(SHARES)]
        product = {(t, b): held.tile([P, tokens], F32, name=f"product{t}{b}") for t in range(BLOCKS) for b in range(BLOCKS)}
        for t in range(BLOCKS):
            for b, cols in pieces[t]:
                listed = offsets[:, cols.start // OFFSETS_PER_COLUMN : cols.stop // OFFSETS_PER_COLUMN]
                looked_up = table[t][:].indirect(listed)
                nc.vector.tensor_tensor(product[t, b][:, cols], looked_up, factor[t, b][:, cols], MULT)
            for k in range(SHARES):
                nc.tensor.matmul(
                    bank[k][:], identity[:], product[t, 0][:, shares[k]], start=(t == 0), stop=(t == BLOCKS - 1)
                )

        turned = [held.tile([P, tokens], F32, name=f"turned{b}") for b in range(BLOCKS)]
        for k in range(SHARES):
            nc.scalar.copy(turned[0][:, shares[k]], bank[k][:])
            nc.sync.dma_start(out[rows(0), shares[k]], turned[0][:, shares[k]])
        for b, cols in ((1, first_half), (1, second_half), (0, left)):
            nc.vector.tensor_tensor(turned[b][:, cols], product[0, b][:, cols], product[1, b][:, cols], ADD)
            nc.scalar.dma_start(out[rows(b), cols], turned[b][:, cols])
